import numpy as np
import ml_dtypes


def mxq(x, axis, fmt="e4m3"):
    dtype, down = {"e4m3": (ml_dtypes.float8_e4m3fn, 7), "e5m2": (ml_dtypes.float8_e5m2, 14)}[fmt]
    v = np.moveaxis(np.asarray(x, np.float32).astype(ml_dtypes.bfloat16).astype(np.float64), axis, -1)
    blocks = v.reshape(v.shape[:-1] + (-1, 32))
    amax = np.abs(blocks).max(-1, keepdims=True)
    byte = np.maximum(np.where(amax > 0, np.frexp(amax)[1] - 1 + 127, 0) - down, 1)
    scale = np.exp2(byte - 127.0)
    codes = (blocks / scale).astype(np.float32).astype(dtype).astype(np.float64)
    return np.moveaxis((codes * scale).reshape(v.shape), -1, axis)


WIDE = False


def mx_kscale(k):
    if not WIDE:
        return np.ones(k)
    levels = np.array([10, -10, 5, -5, 0])
    a = np.random.permutation(np.resize(levels, k // 512 * 4)).reshape(k // 512, 4)
    idx = np.arange(k)
    return np.exp2(a[idx // 512, idx % 128 // 32])


BF16 = ml_dtypes.bfloat16


def bf(x):
    return np.asarray(x, np.float32).astype(BF16)


def f64(x):
    return np.asarray(x).astype(np.float64)


B, I, C, L, O, KW, P = 2, 512, 4, 256, 512, 3, 1


def setup_inputs():
    s = mx_kscale(I)
    return {"x": bf(np.random.standard_normal((B, I, C, L)) * s[None, :, None, None]),
            "time_tensor": bf(np.random.uniform(0.0, 1.0, (B, C, L))),
            "weights": bf(np.random.standard_normal((O, I, C, KW)) / np.sqrt(I * KW) / s[None, :, None, None])}


def reference(x, time_tensor, weights):
    xq = mxq(f64(x).transpose(0, 2, 1, 3), 2, "e4m3")
    wt = f64(weights).transpose(3, 2, 0, 1)
    tp = np.pad(f64(time_tensor), ((0, 0), (0, 0), (P, P)))
    Lw = L + 2 * P - KW + 1
    conv = np.zeros((B, C, O, Lw))
    for j in range(KW):
        y = mxq(wt[j], 2, "e4m3") @ xq
        conv = conv + np.pad(y, ((0, 0), (0, 0), (0, 0), (P, P)))[..., j:j + Lw]
    conv = np.transpose(conv, (0, 2, 1, 3))
    conv = np.pad(conv, ((0, 0), (0, 0), (0, 0), (P, P)))
    out = conv * tp[:, None, :, :]
    return out[..., P:-P]

@@ -1,0 +1,166 @@
+from contextlib import ExitStack
+
+import concourse.mybir as mybir
+from concourse.masks import make_identity
+
+F32 = mybir.dt.float32
+BF16 = mybir.dt.bfloat16
+U32 = mybir.dt.uint32
+U8 = mybir.dt.uint8
+FP8X4 = mybir.dt.float8_e4m3fn_x4
+MULT = mybir.AluOpType.mult
+
+B, I, C, L, O, KW = 2, 512, 4, 256, 512, 3
+P = 128
+PACK = 4
+NOT = O // P
+CK = C * KW
+PAIRS = CK // 2
+R = 4
+JJ = L // R
+PLANES = R + 2
+PLANE_COLS = B * JJ
+XC = PLANES * PLANE_COLS
+FLOPS = 2 * B * O * C * L * I * KW
+
+PINNED = False
+LOADS = (("w", 0), ("x", 0), ("w", 1), ("x", 1), ("w", 2), ("w", 3))
+PESEQ = (
+    ("T", 0, 0), ("T", 0, 1), ("T", 1, 0), ("M", 0, 0), ("T", 1, 1), ("M", 1, 0), ("T", 2, 0), ("M", 0, 1),
+    ("T", 2, 1), ("M", 1, 1), ("T", 3, 0), ("M", 2, 0), ("T", 3, 1), ("M", 2, 1), ("M", 3, 0), ("M", 3, 1),
+)
+
+
+def tile_timeawareconv1d_kernel(tc, x, time_tensor, weights, out):
+    nc = tc.nc
+    with ExitStack() as ctx:
+        if PINNED:
+            ctx.enter_context(tc.manual_schedule())
+        keep = ctx.enter_context(tc.tile_pool(name="keep", bufs=1))
+        wgp = ctx.enter_context(tc.tile_pool(name="wgp", bufs=6))
+        osp = ctx.enter_context(tc.tile_pool(name="osp", bufs=3))
+        tps = ctx.enter_context(tc.psum_pool(name="tps", bufs=6))
+        accp = ctx.enter_context(tc.psum_pool(name="accp", bufs=2))
+
+        ident = keep.tile([P, P], F32)
+        make_identity(nc, ident[:])
+
+        w_raw = [keep.tile([P, I * CK], BF16, name="w_raw%d" % ot) for ot in range(NOT)]
+        x_raw = keep.tile([P, B * PACK * C * L], BF16)
+        xg = keep.tile([P, C * XC * PACK], BF16, align_bytes=64)
+        x_codes = keep.tile([P, C * XC], U32, align_bytes=64)
+        x_scales = keep.tile([P, C * XC], U8, align_bytes=64)
+        w_codes = keep.tile([P, NOT * CK * P], U32, align_bytes=64)
+        w_scales = keep.tile([P, NOT * CK * P], U8, align_bytes=64)
+        tt_sb = keep.tile([P, B * C * L], BF16)
+
+        xr_dma = x_raw[:].rearrange("p (b j c l) -> p b j c l", b=B, j=PACK, c=C)
+        xr_cp = x_raw[:].rearrange("p (b j c jj r) -> p b c jj j r", b=B, j=PACK, c=C, r=R)
+        xg6 = xg[:].rearrange("p (c q b jj t) -> p c q b jj t", c=C, q=PLANES, b=B, t=PACK)
+        wv = [w_raw[ot][:].bitcast(F32).rearrange("o (p j m) -> o p j m", j=PACK, m=PAIRS) for ot in range(NOT)]
+        tt4 = tt_sb[:].rearrange("p (b c jj r) -> p b c jj r", b=B, c=C, r=R)
+        out_v = out.rearrange("b (t p) c l -> t p b (c l)", p=P)
+
+        nc.vector.memset(xg6[:, :, 0, :, 0, :], 0.0)
+        nc.vector.memset(xg6[:, :, PLANES - 1, :, JJ - 1, :], 0.0)
+
+        for kind, n in LOADS:
+            if kind == "w":
+                nc.sync.dma_start(
+                    out=w_raw[n][:], in_=weights[n * P:(n + 1) * P].rearrange("o i c k -> o (i c k)")
+                )
+            else:
+                for b in range(B):
+                    nc.sync.dma_start(
+                        out=xr_dma[:, b, :, 2 * n:2 * n + 2, :].rearrange("p j c l -> p j (c l)"),
+                        in_=x[b].rearrange("(p j) c l -> p j c l", j=PACK)[:, :, 2 * n:2 * n + 2, :].rearrange(
+                            "p j c l -> p j (c l)"
+                        ),
+                    )
+        nc.scalar.dma_start(out=tt_sb[:], in_=time_tensor.rearrange("b c l -> (b c l)").partition_broadcast(P))
+
+        def x_work(h):
+            cs = slice(2 * h, 2 * h + 2)
+            for b in range(B):
+                nc.vector.tensor_copy(
+                    out=xg6[:, cs, 1:1 + R, b, :, :].rearrange("p c q jj t -> p c jj t q"),
+                    in_=xr_cp[:, b, cs],
+                )
+            nc.vector.tensor_copy(out=xg6[:, cs, 0, :, 1:JJ, :], in_=xg6[:, cs, R, :, 0:JJ - 1, :])
+            nc.vector.tensor_copy(out=xg6[:, cs, PLANES - 1, :, 0:JJ - 1, :], in_=xg6[:, cs, 1, :, 1:JJ, :])
+            for c in (2 * h, 2 * h + 1):
+                for lo, n in ((0, 512), (512, 256)):
+                    a = c * XC + lo
+                    nc.vector.quantize_mx(
+                        out=x_codes[:, a:a + n].bitcast(FP8X4),
+                        scales=x_scales[:, a:a + n],
+                        in_=xg[:, a * PACK:(a + n) * PACK],
+                    )
+
+        def t_unit(ot, h):
+            banks = []
+            for mi in range(3):
+                m = 3 * h + mi
+                tp = tps.tile([P, PACK * P], F32, name="tp")
+                for j in range(PACK):
+                    nc.tensor.transpose(out=tp[:, j * P:(j + 1) * P], in_=wv[ot][:, :, j, m], identity=ident[:])
+                banks.append(tp)
+            groups = []
+            for mi in range(3):
+                wg = wgp.tile([P, 2 * P * PACK], BF16, name="wg", align_bytes=64)
+                nc.scalar.copy(
+                    out=wg[:].rearrange("p (e o t) -> p e o t", e=2, t=PACK),
+                    in_=banks[mi][:].bitcast(BF16).rearrange("p (t o e) -> p e o t", t=PACK, e=2),
+                )
+                groups.append(wg)
+            for mi in range(3):
+                a = (ot * CK + 2 * (3 * h + mi)) * P
+                nc.vector.quantize_mx(
+                    out=w_codes[:, a:a + 2 * P].bitcast(FP8X4),
+                    scales=w_scales[:, a:a + 2 * P],
+                    in_=groups[mi][:],
+                )
+
+        def m_unit(ot, h):
+            accs = []
+            for cc in range(2):
+                c = 2 * h + cc
+                acc = accp.tile([P, R * PLANE_COLS], F32, name="acc")
+                for k in range(KW):
+                    a = (ot * CK + c * KW + k) * P
+                    xa = c * XC + k * PLANE_COLS
+                    nc.tensor.matmul_mx(
+                        out=acc[:],
+                        lhsT=w_codes[:, a:a + P].bitcast(FP8X4),
+                        lhsT_scale=w_scales[:, a:a + P],
+                        rhs=x_codes[:, xa:xa + R * PLANE_COLS].bitcast(FP8X4),
+                        rhs_scale=x_scales[:, xa:xa + R * PLANE_COLS],
+                        start=(k == 0),
+                        stop=(k == KW - 1),
+                    )
+                accs.append(acc)
+            o_sb = osp.tile([P, B * 2 * L], F32, name="o_sb")
+            o5 = o_sb[:].rearrange("p (b c jj r) -> p b c jj r", b=B, c=2, r=R)
+            for cc in range(2):
+                nc.vector.tensor_tensor(
+                    out=o5[:, :, cc],
+                    in0=accs[cc][:].rearrange("p (r b jj) -> p b jj r", r=R, b=B),
+                    in1=tt4[:, :, 2 * h + cc],
+                    op=MULT,
+                )
+            nc.sync.dma_start(
+                out=out_v[ot][:, :, h * 2 * L:(h + 1) * 2 * L],
+                in_=o_sb[:].rearrange("p (b n) -> p b n", b=B),
+            )
+
+        seq = PESEQ
+        x_done = set()
+        for idx, (kind, ot, h) in enumerate(seq):
+            for k2, o2, h2 in seq[idx:idx + 3]:
+                if k2 == "M" and h2 not in x_done:
+                    x_work(h2)
+                    x_done.add(h2)
+            if kind == "T":
+                t_unit(ot, h)
+            else:
+                m_unit(ot, h)

@@ -5,6 +5,7 @@ from concourse.masks import make_identity
 
 F32 = mybir.dt.float32
 BF16 = mybir.dt.bfloat16
+I32 = mybir.dt.int32
 U32 = mybir.dt.uint32
 U8 = mybir.dt.uint8
 FP8X4 = mybir.dt.float8_e4m3fn_x4
@@ -21,14 +22,17 @@ JJ = L // R
 PLANES = R + 2
 PLANE_COLS = B * JJ
 XC = PLANES * PLANE_COLS
+BANK = 512
 FLOPS = 2 * B * O * C * L * I * KW
 
-PINNED = False
+PINNED = True
 LOADS = (("w", 0), ("x", 0), ("w", 1), ("x", 1), ("w", 2), ("w", 3))
 PESEQ = (
     ("T", 0, 0), ("T", 0, 1), ("T", 1, 0), ("M", 0, 0), ("T", 1, 1), ("M", 1, 0), ("T", 2, 0), ("M", 0, 1),
     ("T", 2, 1), ("M", 1, 1), ("T", 3, 0), ("M", 2, 0), ("T", 3, 1), ("M", 2, 1), ("M", 3, 0), ("M", 3, 1),
 )
+XPOS = ((0, 1, 2), (3, 4, 5))
+QW_LAG = 1
 
 
 def tile_timeawareconv1d_kernel(tc, x, time_tensor, weights, out):
@@ -37,13 +41,10 @@ def tile_timeawareconv1d_kernel(tc, x, time_tensor, weights, out):
         if PINNED:
             ctx.enter_context(tc.manual_schedule())
         keep = ctx.enter_context(tc.tile_pool(name="keep", bufs=1))
-        wgp = ctx.enter_context(tc.tile_pool(name="wgp", bufs=6))
-        osp = ctx.enter_context(tc.tile_pool(name="osp", bufs=3))
+        wgp = ctx.enter_context(tc.tile_pool(name="wgp", bufs=9))
+        osp = ctx.enter_context(tc.tile_pool(name="osp", bufs=4))
         tps = ctx.enter_context(tc.psum_pool(name="tps", bufs=6))
         accp = ctx.enter_context(tc.psum_pool(name="accp", bufs=2))
-
-        ident = keep.tile([P, P], F32)
-        make_identity(nc, ident[:])
 
         w_raw = [keep.tile([P, I * CK], BF16, name="w_raw%d" % ot) for ot in range(NOT)]
         x_raw = keep.tile([P, B * PACK * C * L], BF16)
@@ -52,7 +53,10 @@ def tile_timeawareconv1d_kernel(tc, x, time_tensor, weights, out):
         x_scales = keep.tile([P, C * XC], U8, align_bytes=64)
         w_codes = keep.tile([P, NOT * CK * P], U32, align_bytes=64)
         w_scales = keep.tile([P, NOT * CK * P], U8, align_bytes=64)
+        tt_row = keep.tile([P, B * C * L], BF16)
         tt_sb = keep.tile([P, B * C * L], BF16)
+        ones = keep.tile([P, P], BF16)
+        ident = keep.tile([P, P], F32)
 
         xr_dma = x_raw[:].rearrange("p (b j c l) -> p b j c l", b=B, j=PACK, c=C)
         xr_cp = x_raw[:].rearrange("p (b j c jj r) -> p b c jj j r", b=B, j=PACK, c=C, r=R)
@@ -61,9 +65,9 @@ def tile_timeawareconv1d_kernel(tc, x, time_tensor, weights, out):
         tt4 = tt_sb[:].rearrange("p (b c jj r) -> p b c jj r", b=B, c=C, r=R)
         out_v = out.rearrange("b (t p) c l -> t p b (c l)", p=P)
 
-        nc.vector.memset(xg6[:, :, 0, :, 0, :], 0.0)
-        nc.vector.memset(xg6[:, :, PLANES - 1, :, JJ - 1, :], 0.0)
-
+        nc.scalar.dma_start(out=tt_row[0:32, :], in_=time_tensor.rearrange("b c l -> (b c l)").partition_broadcast(32))
+        nc.vector.memset(tt_row[32:64, :].bitcast(I32), 0)
+        nc.vector.memset(tt_row[64:128, :].bitcast(I32), 0)
         for kind, n in LOADS:
             if kind == "w":
                 nc.sync.dma_start(
@@ -77,17 +81,34 @@ def tile_timeawareconv1d_kernel(tc, x, time_tensor, weights, out):
                             "p j c l -> p j (c l)"
                         ),
                     )
-        nc.scalar.dma_start(out=tt_sb[:], in_=time_tensor.rearrange("b c l -> (b c l)").partition_broadcast(P))
+        make_identity(nc, ident[:])
+        nc.vector.memset(ones[:], 0.0)
+        nc.vector.memset(ones[0:1, :], 1.0)
+        nc.vector.memset(xg6[:, :, 0, :, 0, :], 0.0)
+        nc.vector.memset(xg6[:, :, PLANES - 1, :, JJ - 1, :], 0.0)
+        for q in range(B * C * L // BANK):
+            tb = tps.tile([P, BANK], F32, name="tp")
+            nc.tensor.matmul(out=tb[:], lhsT=ones[:], rhs=tt_row[:, q * BANK:(q + 1) * BANK], start=True, stop=True)
+            if q % 2 == 0:
+                nc.scalar.copy(out=tt_sb[:, q * BANK:(q + 1) * BANK], in_=tb[:])
+            else:
+                nc.vector.tensor_copy(out=tt_sb[:, q * BANK:(q + 1) * BANK], in_=tb[:])
 
-        def x_work(h):
+        def x_regroup(h):
             cs = slice(2 * h, 2 * h + 2)
             for b in range(B):
-                nc.vector.tensor_copy(
-                    out=xg6[:, cs, 1:1 + R, b, :, :].rearrange("p c q jj t -> p c jj t q"),
-                    in_=xr_cp[:, b, cs],
-                )
+                for rp in range(0, R, 2):
+                    nc.vector.tensor_copy(
+                        out=xg6[:, cs, 1 + rp:3 + rp, b, :, :].rearrange("p c q jj t -> p c jj t q"),
+                        in_=xr_cp[:, b, cs, :, :, rp:rp + 2],
+                    )
+
+        def x_edges(h):
+            cs = slice(2 * h, 2 * h + 2)
             nc.vector.tensor_copy(out=xg6[:, cs, 0, :, 1:JJ, :], in_=xg6[:, cs, R, :, 0:JJ - 1, :])
             nc.vector.tensor_copy(out=xg6[:, cs, PLANES - 1, :, 0:JJ - 1, :], in_=xg6[:, cs, 1, :, 1:JJ, :])
+
+        def x_quant(h):
             for c in (2 * h, 2 * h + 1):
                 for lo, n in ((0, 512), (512, 256)):
                     a = c * XC + lo
@@ -101,7 +122,7 @@ def tile_timeawareconv1d_kernel(tc, x, time_tensor, weights, out):
             banks = []
             for mi in range(3):
                 m = 3 * h + mi
-                tp = tps.tile([P, PACK * P], F32, name="tp")
+                tp = tps.tile([P, BANK], F32, name="tp")
                 for j in range(PACK):
                     nc.tensor.transpose(out=tp[:, j * P:(j + 1) * P], in_=wv[ot][:, :, j, m], identity=ident[:])
                 banks.append(tp)
@@ -113,6 +134,9 @@ def tile_timeawareconv1d_kernel(tc, x, time_tensor, weights, out):
                     in_=banks[mi][:].bitcast(BF16).rearrange("p (t o e) -> p e o t", t=PACK, e=2),
                 )
                 groups.append(wg)
+            return groups
+
+        def w_quant(ot, h, groups):
             for mi in range(3):
                 a = (ot * CK + 2 * (3 * h + mi)) * P
                 nc.vector.quantize_mx(
@@ -125,7 +149,7 @@ def tile_timeawareconv1d_kernel(tc, x, time_tensor, weights, out):
             accs = []
             for cc in range(2):
                 c = 2 * h + cc
-                acc = accp.tile([P, R * PLANE_COLS], F32, name="acc")
+                acc = accp.tile([P, BANK], F32, name="acc")
                 for k in range(KW):
                     a = (ot * CK + c * KW + k) * P
                     xa = c * XC + k * PLANE_COLS
@@ -133,8 +157,8 @@ def tile_timeawareconv1d_kernel(tc, x, time_tensor, weights, out):
                         out=acc[:],
                         lhsT=w_codes[:, a:a + P].bitcast(FP8X4),
                         lhsT_scale=w_scales[:, a:a + P],
-                        rhs=x_codes[:, xa:xa + R * PLANE_COLS].bitcast(FP8X4),
-                        rhs_scale=x_scales[:, xa:xa + R * PLANE_COLS],
+                        rhs=x_codes[:, xa:xa + BANK].bitcast(FP8X4),
+                        rhs_scale=x_scales[:, xa:xa + BANK],
                         start=(k == 0),
                         stop=(k == KW - 1),
                     )
@@ -153,14 +177,19 @@ def tile_timeawareconv1d_kernel(tc, x, time_tensor, weights, out):
                 in_=o_sb[:].rearrange("p (b n) -> p b n", b=B),
             )
 
-        seq = PESEQ
-        x_done = set()
-        for idx, (kind, ot, h) in enumerate(seq):
-            for k2, o2, h2 in seq[idx:idx + 3]:
-                if k2 == "M" and h2 not in x_done:
-                    x_work(h2)
-                    x_done.add(h2)
+        waiting = []
+        for idx, (kind, ot, h) in enumerate(PESEQ):
+            for hh in range(2):
+                if XPOS[hh][0] == idx:
+                    x_regroup(hh)
+                if XPOS[hh][1] == idx:
+                    x_edges(hh)
+                if XPOS[hh][2] == idx:
+                    x_quant(hh)
             if kind == "T":
-                t_unit(ot, h)
+                waiting.append((idx, ot, h, t_unit(ot, h)))
             else:
                 m_unit(ot, h)
+            while waiting and waiting[0][0] <= idx - QW_LAG:
+                w_quant(waiting[0][1], waiting[0][2], waiting[0][3])
+                waiting = waiting[1:]

@@ -25,21 +25,21 @@ XC = PLANES * PLANE_COLS
 BANK = 512
 FLOPS = 2 * B * O * C * L * I * KW
 
-PINNED = True
 LOADS = (("w", 0), ("x", 0), ("w", 1), ("x", 1), ("w", 2), ("w", 3))
-PESEQ = (
-    ("T", 0, 0), ("T", 0, 1), ("T", 1, 0), ("M", 0, 0), ("T", 1, 1), ("M", 1, 0), ("T", 2, 0), ("M", 0, 1),
-    ("T", 2, 1), ("M", 1, 1), ("T", 3, 0), ("M", 2, 0), ("T", 3, 1), ("M", 2, 1), ("M", 3, 0), ("M", 3, 1),
+STEPS = (
+    ((0, 0), None), ((0, 1), None), ((1, 0), (0, 0)), ((1, 1), (1, 0)), ((2, 0), (0, 1)),
+    ((2, 1), (1, 1)), ((3, 0), (2, 0)), ((3, 1), (2, 1)), (None, (3, 0)), (None, (3, 1)),
 )
-XPOS = ((0, 1, 2), (3, 4, 5))
-QW_LAG = 1
+XPLACE = (
+    ((0, 0), (0, 2), (0, 4), (0, 4), (0, 5), (0, 5)),
+    ((1, 4), (1, 4), (2, 2), (3, 0), (3, 2), (3, 3)),
+)
 
 
 def tile_timeawareconv1d_kernel(tc, x, time_tensor, weights, out):
     nc = tc.nc
     with ExitStack() as ctx:
-        if PINNED:
-            ctx.enter_context(tc.manual_schedule())
+        ctx.enter_context(tc.manual_schedule())
         keep = ctx.enter_context(tc.tile_pool(name="keep", bufs=1))
         wgp = ctx.enter_context(tc.tile_pool(name="wgp", bufs=9))
         osp = ctx.enter_context(tc.tile_pool(name="osp", bufs=4))
@@ -55,7 +55,7 @@ def tile_timeawareconv1d_kernel(tc, x, time_tensor, weights, out):
         w_scales = keep.tile([P, NOT * CK * P], U8, align_bytes=64)
         tt_row = keep.tile([P, B * C * L], BF16)
         tt_sb = keep.tile([P, B * C * L], BF16)
-        ones = keep.tile([P, P], BF16)
+        sel = keep.tile([P, P], BF16)
         ident = keep.tile([P, P], F32)
 
         xr_dma = x_raw[:].rearrange("p (b j c l) -> p b j c l", b=B, j=PACK, c=C)
@@ -65,9 +65,7 @@ def tile_timeawareconv1d_kernel(tc, x, time_tensor, weights, out):
         tt4 = tt_sb[:].rearrange("p (b c jj r) -> p b c jj r", b=B, c=C, r=R)
         out_v = out.rearrange("b (t p) c l -> t p b (c l)", p=P)
 
-        nc.scalar.dma_start(out=tt_row[0:32, :], in_=time_tensor.rearrange("b c l -> (b c l)").partition_broadcast(32))
-        nc.vector.memset(tt_row[32:64, :].bitcast(I32), 0)
-        nc.vector.memset(tt_row[64:128, :].bitcast(I32), 0)
+        nc.sync.dma_start(out=tt_row[0:32, :], in_=time_tensor.rearrange("b c l -> (b c l)").partition_broadcast(32))
         for kind, n in LOADS:
             if kind == "w":
                 nc.sync.dma_start(
@@ -81,50 +79,50 @@ def tile_timeawareconv1d_kernel(tc, x, time_tensor, weights, out):
                             "p j c l -> p j (c l)"
                         ),
                     )
+        nc.vector.memset(tt_row[32:64, :].bitcast(I32), 0)
+        nc.vector.memset(tt_row[64:128, :].bitcast(I32), 0)
+        nc.vector.memset(sel[:], 0.0)
+        nc.vector.memset(sel[0:1, :], 1.0)
         make_identity(nc, ident[:])
-        nc.vector.memset(ones[:], 0.0)
-        nc.vector.memset(ones[0:1, :], 1.0)
         nc.vector.memset(xg6[:, :, 0, :, 0, :], 0.0)
         nc.vector.memset(xg6[:, :, PLANES - 1, :, JJ - 1, :], 0.0)
         for q in range(B * C * L // BANK):
             tb = tps.tile([P, BANK], F32, name="tp")
-            nc.tensor.matmul(out=tb[:], lhsT=ones[:], rhs=tt_row[:, q * BANK:(q + 1) * BANK], start=True, stop=True)
+            nc.tensor.matmul(out=tb[:], lhsT=sel[:], rhs=tt_row[:, q * BANK:(q + 1) * BANK], start=True, stop=True)
             if q % 2 == 0:
                 nc.scalar.copy(out=tt_sb[:, q * BANK:(q + 1) * BANK], in_=tb[:])
             else:
                 nc.vector.tensor_copy(out=tt_sb[:, q * BANK:(q + 1) * BANK], in_=tb[:])
 
-        def x_regroup(h):
+        def x_piece(h, piece):
             cs = slice(2 * h, 2 * h + 2)
-            for b in range(B):
+            if piece < 2:
                 for rp in range(0, R, 2):
                     nc.vector.tensor_copy(
-                        out=xg6[:, cs, 1 + rp:3 + rp, b, :, :].rearrange("p c q jj t -> p c jj t q"),
-                        in_=xr_cp[:, b, cs, :, :, rp:rp + 2],
+                        out=xg6[:, cs, 1 + rp:3 + rp, piece, :, :].rearrange("p c q jj t -> p c jj t q"),
+                        in_=xr_cp[:, piece, cs, :, :, rp:rp + 2],
                     )
-
-        def x_edges(h):
-            cs = slice(2 * h, 2 * h + 2)
-            nc.vector.tensor_copy(out=xg6[:, cs, 0, :, 1:JJ, :], in_=xg6[:, cs, R, :, 0:JJ - 1, :])
-            nc.vector.tensor_copy(out=xg6[:, cs, PLANES - 1, :, 0:JJ - 1, :], in_=xg6[:, cs, 1, :, 1:JJ, :])
-
-        def x_quant(h):
-            for c in (2 * h, 2 * h + 1):
+            elif piece == 2:
+                nc.vector.tensor_copy(out=xg6[:, cs, 0, :, 1:JJ, :], in_=xg6[:, cs, R, :, 0:JJ - 1, :])
+            elif piece == 3:
+                nc.vector.tensor_copy(out=xg6[:, cs, PLANES - 1, :, 0:JJ - 1, :], in_=xg6[:, cs, 1, :, 1:JJ, :])
+            else:
                 for lo, n in ((0, 512), (512, 256)):
-                    a = c * XC + lo
+                    a = (2 * h + piece - 4) * XC + lo
                     nc.vector.quantize_mx(
                         out=x_codes[:, a:a + n].bitcast(FP8X4),
                         scales=x_scales[:, a:a + n],
                         in_=xg[:, a * PACK:(a + n) * PACK],
                     )
 
-        def t_unit(ot, h):
+        def transposes(ot, h):
             banks = []
             for mi in range(3):
-                m = 3 * h + mi
                 tp = tps.tile([P, BANK], F32, name="tp")
                 for j in range(PACK):
-                    nc.tensor.transpose(out=tp[:, j * P:(j + 1) * P], in_=wv[ot][:, :, j, m], identity=ident[:])
+                    nc.tensor.transpose(
+                        out=tp[:, j * P:(j + 1) * P], in_=wv[ot][:, :, j, 3 * h + mi], identity=ident[:]
+                    )
                 banks.append(tp)
             groups = []
             for mi in range(3):
@@ -136,16 +134,13 @@ def tile_timeawareconv1d_kernel(tc, x, time_tensor, weights, out):
                 groups.append(wg)
             return groups
 
-        def w_quant(ot, h, groups):
-            for mi in range(3):
-                a = (ot * CK + 2 * (3 * h + mi)) * P
-                nc.vector.quantize_mx(
-                    out=w_codes[:, a:a + 2 * P].bitcast(FP8X4),
-                    scales=w_scales[:, a:a + 2 * P],
-                    in_=groups[mi][:],
-                )
+        def w_quant(ot, h, mi, wg):
+            a = (ot * CK + 2 * (3 * h + mi)) * P
+            nc.vector.quantize_mx(
+                out=w_codes[:, a:a + 2 * P].bitcast(FP8X4), scales=w_scales[:, a:a + 2 * P], in_=wg[:]
+            )
 
-        def m_unit(ot, h):
+        def passes(ot, h):
             accs = []
             for cc in range(2):
                 c = 2 * h + cc
@@ -163,33 +158,36 @@ def tile_timeawareconv1d_kernel(tc, x, time_tensor, weights, out):
                         stop=(k == KW - 1),
                     )
                 accs.append(acc)
-            o_sb = osp.tile([P, B * 2 * L], F32, name="o_sb")
-            o5 = o_sb[:].rearrange("p (b c jj r) -> p b c jj r", b=B, c=2, r=R)
-            for cc in range(2):
-                nc.vector.tensor_tensor(
-                    out=o5[:, :, cc],
-                    in0=accs[cc][:].rearrange("p (r b jj) -> p b jj r", r=R, b=B),
-                    in1=tt4[:, :, 2 * h + cc],
-                    op=MULT,
-                )
-            nc.sync.dma_start(
-                out=out_v[ot][:, :, h * 2 * L:(h + 1) * 2 * L],
-                in_=o_sb[:].rearrange("p (b n) -> p b n", b=B),
-            )
+            return accs
 
-        waiting = []
-        for idx, (kind, ot, h) in enumerate(PESEQ):
-            for hh in range(2):
-                if XPOS[hh][0] == idx:
-                    x_regroup(hh)
-                if XPOS[hh][1] == idx:
-                    x_edges(hh)
-                if XPOS[hh][2] == idx:
-                    x_quant(hh)
-            if kind == "T":
-                waiting.append((idx, ot, h, t_unit(ot, h)))
-            else:
-                m_unit(ot, h)
-            while waiting and waiting[0][0] <= idx - QW_LAG:
-                w_quant(waiting[0][1], waiting[0][2], waiting[0][3])
-                waiting = waiting[1:]
+        for step, (tu, mu) in enumerate(STEPS):
+            groups = transposes(tu[0], tu[1]) if tu else None
+            accs = passes(mu[0], mu[1]) if mu else None
+            last = step == len(STEPS) - 1
+            if mu:
+                o_sb = osp.tile([P, B * 2 * L], F32, name="o_sb")
+                o5 = o_sb[:].rearrange("p (b c jj r) -> p b c jj r", b=B, c=2, r=R)
+                o4 = o_sb[:].rearrange("p (b c l) -> p b c l", b=B, c=2)
+            for slot in range(6):
+                for h in range(2):
+                    for piece in range(6):
+                        if XPLACE[h][piece] == (step, slot):
+                            x_piece(h, piece)
+                if slot % 2 == 0 and slot < 5 and tu:
+                    w_quant(tu[0], tu[1], slot // 2, groups[slot // 2])
+                if slot % 2 == 1 and slot < 5 and mu:
+                    cc = slot // 2
+                    c = 2 * mu[1] + cc
+                    nc.vector.tensor_tensor(
+                        out=o5[:, :, cc],
+                        in0=accs[cc][:].rearrange("p (r b jj) -> p b jj r", r=R, b=B),
+                        in1=tt4[:, :, c],
+                        op=MULT,
+                    )
+                    if last:
+                        nc.sync.dma_start(out=out_v[mu[0]][:, :, c * L:(c + 1) * L], in_=o4[:, :, cc, :])
+            if mu and not last:
+                nc.sync.dma_start(
+                    out=out_v[mu[0]][:, :, mu[1] * 2 * L:(mu[1] + 1) * 2 * L],
+                    in_=o_sb[:].rearrange("p (b n) -> p b n", b=B),
+                )

@@ -26,13 +26,15 @@ BANK = 512
 FLOPS = 2 * B * O * C * L * I * KW
 
 LOADS = (("w", 0), ("x", 0), ("w", 1), ("x", 1), ("w", 2), ("w", 3))
-STEPS = (
-    ((0, 0), None), ((0, 1), None), ((1, 0), (0, 0)), ((1, 1), (1, 0)), ((2, 0), (0, 1)),
-    ((2, 1), (1, 1)), ((3, 0), (2, 0)), ((3, 1), (2, 1)), (None, (3, 0)), (None, (3, 1)),
+PESEQ = (
+    "T00", "T01", "T10", "M00", "T11", "T20", "M10", "T21", "T30", "M01", "M11", "T31", "M20", "M21", "M30", "M31",
 )
-XPLACE = (
-    ((0, 0), (0, 2), (0, 4), (0, 4), (0, 5), (0, 5)),
-    ((1, 4), (1, 4), (2, 2), (3, 0), (3, 2), (3, 3)),
+VSEQ = (
+    "XR00", "XR10", "QW000", "QW001", "XE00", "XE10", "QW002", "QX0", "QX1", "XR01", "XR11", "EV000", "EV001",
+    "QW100", "QW101", "XE01", "XE11", "QW102", "CO201", "QW010", "QW011", "EV100", "EV101", "QW012", "QX2", "QX3",
+    "QW110", "QW111", "CO301", "QW112", "EV010", "QW200", "EV011", "QW201", "EV110", "QW202", "EV111", "QW210",
+    "QW211", "QW212", "QW300", "QW301", "QW302", "QW310", "EV200", "EV201", "QW311", "EV210", "QW312", "EV211",
+    "EV300", "EV301", "EV310", "EV311",
 )
 
 
@@ -41,13 +43,12 @@ def tile_timeawareconv1d_kernel(tc, x, time_tensor, weights, out):
     with ExitStack() as ctx:
         ctx.enter_context(tc.manual_schedule())
         keep = ctx.enter_context(tc.tile_pool(name="keep", bufs=1))
-        wgp = ctx.enter_context(tc.tile_pool(name="wgp", bufs=9))
-        osp = ctx.enter_context(tc.tile_pool(name="osp", bufs=4))
-        tps = ctx.enter_context(tc.psum_pool(name="tps", bufs=6))
-        accp = ctx.enter_context(tc.psum_pool(name="accp", bufs=2))
+        wgp = ctx.enter_context(tc.tile_pool(name="wgp", bufs=24))
+        osp = ctx.enter_context(tc.tile_pool(name="osp", bufs=8))
+        psum = ctx.enter_context(tc.psum_pool(name="psum", bufs=8))
 
         w_raw = [keep.tile([P, I * CK], BF16, name="w_raw%d" % ot) for ot in range(NOT)]
-        x_raw = keep.tile([P, B * PACK * C * L], BF16)
+        x_raw = [[keep.tile([P, PACK * 2 * L], BF16, name="x_raw%d%d" % (b, h)) for h in range(2)] for b in range(B)]
         xg = keep.tile([P, C * XC * PACK], BF16, align_bytes=64)
         x_codes = keep.tile([P, C * XC], U32, align_bytes=64)
         x_scales = keep.tile([P, C * XC], U8, align_bytes=64)
@@ -58,8 +59,6 @@ def tile_timeawareconv1d_kernel(tc, x, time_tensor, weights, out):
         sel = keep.tile([P, P], BF16)
         ident = keep.tile([P, P], F32)
 
-        xr_dma = x_raw[:].rearrange("p (b j c l) -> p b j c l", b=B, j=PACK, c=C)
-        xr_cp = x_raw[:].rearrange("p (b j c jj r) -> p b c jj j r", b=B, j=PACK, c=C, r=R)
         xg6 = xg[:].rearrange("p (c q b jj t) -> p c q b jj t", c=C, q=PLANES, b=B, t=PACK)
         wv = [w_raw[ot][:].bitcast(F32).rearrange("o (p j m) -> o p j m", j=PACK, m=PAIRS) for ot in range(NOT)]
         tt4 = tt_sb[:].rearrange("p (b c jj r) -> p b c jj r", b=B, c=C, r=R)
@@ -74,7 +73,7 @@ def tile_timeawareconv1d_kernel(tc, x, time_tensor, weights, out):
             else:
                 for b in range(B):
                     nc.sync.dma_start(
-                        out=xr_dma[:, b, :, 2 * n:2 * n + 2, :].rearrange("p j c l -> p j (c l)"),
+                        out=x_raw[b][n][:].rearrange("p (j n) -> p j n", j=PACK),
                         in_=x[b].rearrange("(p j) c l -> p j c l", j=PACK)[:, :, 2 * n:2 * n + 2, :].rearrange(
                             "p j c l -> p j (c l)"
                         ),
@@ -87,64 +86,73 @@ def tile_timeawareconv1d_kernel(tc, x, time_tensor, weights, out):
         nc.vector.memset(xg6[:, :, 0, :, 0, :], 0.0)
         nc.vector.memset(xg6[:, :, PLANES - 1, :, JJ - 1, :], 0.0)
         for q in range(B * C * L // BANK):
-            tb = tps.tile([P, BANK], F32, name="tp")
+            tb = psum.tile([P, BANK], F32, name="bank")
             nc.tensor.matmul(out=tb[:], lhsT=sel[:], rhs=tt_row[:, q * BANK:(q + 1) * BANK], start=True, stop=True)
             if q % 2 == 0:
                 nc.scalar.copy(out=tt_sb[:, q * BANK:(q + 1) * BANK], in_=tb[:])
             else:
                 nc.vector.tensor_copy(out=tt_sb[:, q * BANK:(q + 1) * BANK], in_=tb[:])
 
-        def x_piece(h, piece):
+        banks = {}
+        groups = {}
+        accs = {}
+        done = set()
+
+        def x_regroup(b, h):
             cs = slice(2 * h, 2 * h + 2)
-            if piece < 2:
-                for rp in range(0, R, 2):
-                    nc.vector.tensor_copy(
-                        out=xg6[:, cs, 1 + rp:3 + rp, piece, :, :].rearrange("p c q jj t -> p c jj t q"),
-                        in_=xr_cp[:, piece, cs, :, :, rp:rp + 2],
-                    )
-            elif piece == 2:
+            for rp in range(0, R, 2):
+                nc.vector.tensor_copy(
+                    out=xg6[:, cs, 1 + rp:3 + rp, b, :, :].rearrange("p c q jj t -> p c jj t q"),
+                    in_=x_raw[b][h][:].rearrange("p (j c jj r) -> p c jj j r", j=PACK, c=2, r=R)[:, :, :, :, rp:rp + 2],
+                )
+
+        def x_edge(side, h):
+            cs = slice(2 * h, 2 * h + 2)
+            if side == 0:
                 nc.vector.tensor_copy(out=xg6[:, cs, 0, :, 1:JJ, :], in_=xg6[:, cs, R, :, 0:JJ - 1, :])
-            elif piece == 3:
-                nc.vector.tensor_copy(out=xg6[:, cs, PLANES - 1, :, 0:JJ - 1, :], in_=xg6[:, cs, 1, :, 1:JJ, :])
             else:
-                for lo, n in ((0, 512), (512, 256)):
-                    a = (2 * h + piece - 4) * XC + lo
-                    nc.vector.quantize_mx(
-                        out=x_codes[:, a:a + n].bitcast(FP8X4),
-                        scales=x_scales[:, a:a + n],
-                        in_=xg[:, a * PACK:(a + n) * PACK],
-                    )
+                nc.vector.tensor_copy(out=xg6[:, cs, PLANES - 1, :, 0:JJ - 1, :], in_=xg6[:, cs, 1, :, 1:JJ, :])
+
+        def x_quant(c):
+            for lo, n in ((0, 512), (512, 256)):
+                a = c * XC + lo
+                nc.vector.quantize_mx(
+                    out=x_codes[:, a:a + n].bitcast(FP8X4),
+                    scales=x_scales[:, a:a + n],
+                    in_=xg[:, a * PACK:(a + n) * PACK],
+                )
 
         def transposes(ot, h):
-            banks = []
             for mi in range(3):
-                tp = tps.tile([P, BANK], F32, name="tp")
+                tp = psum.tile([P, BANK], F32, name="bank")
                 for j in range(PACK):
                     nc.tensor.transpose(
                         out=tp[:, j * P:(j + 1) * P], in_=wv[ot][:, :, j, 3 * h + mi], identity=ident[:]
                     )
-                banks.append(tp)
-            groups = []
-            for mi in range(3):
-                wg = wgp.tile([P, 2 * P * PACK], BF16, name="wg", align_bytes=64)
-                nc.scalar.copy(
-                    out=wg[:].rearrange("p (e o t) -> p e o t", e=2, t=PACK),
-                    in_=banks[mi][:].bitcast(BF16).rearrange("p (t o e) -> p e o t", t=PACK, e=2),
-                )
-                groups.append(wg)
-            return groups
+                banks[(ot, h, mi)] = tp
 
-        def w_quant(ot, h, mi, wg):
+        def copy_out(on_vector, ot, h, mi):
+            wg = wgp.tile([P, 2 * P * PACK], BF16, name="wg", align_bytes=64)
+            dst = wg[:].rearrange("p (e o t) -> p e o t", e=2, t=PACK)
+            src = banks[(ot, h, mi)][:].bitcast(BF16).rearrange("p (t o e) -> p e o t", t=PACK, e=2)
+            if on_vector:
+                nc.vector.tensor_copy(out=dst, in_=src)
+            else:
+                nc.scalar.copy(out=dst, in_=src)
+            groups[(ot, h, mi)] = wg
+
+        def w_quant(ot, h, mi):
             a = (ot * CK + 2 * (3 * h + mi)) * P
             nc.vector.quantize_mx(
-                out=w_codes[:, a:a + 2 * P].bitcast(FP8X4), scales=w_scales[:, a:a + 2 * P], in_=wg[:]
+                out=w_codes[:, a:a + 2 * P].bitcast(FP8X4),
+                scales=w_scales[:, a:a + 2 * P],
+                in_=groups[(ot, h, mi)][:],
             )
 
         def passes(ot, h):
-            accs = []
             for cc in range(2):
                 c = 2 * h + cc
-                acc = accp.tile([P, BANK], F32, name="acc")
+                acc = psum.tile([P, BANK], F32, name="bank")
                 for k in range(KW):
                     a = (ot * CK + c * KW + k) * P
                     xa = c * XC + k * PLANE_COLS
@@ -157,37 +165,68 @@ def tile_timeawareconv1d_kernel(tc, x, time_tensor, weights, out):
                         start=(k == 0),
                         stop=(k == KW - 1),
                     )
-                accs.append(acc)
-            return accs
+                accs[(ot, h, cc)] = acc
 
-        for step, (tu, mu) in enumerate(STEPS):
-            groups = transposes(tu[0], tu[1]) if tu else None
-            accs = passes(mu[0], mu[1]) if mu else None
-            last = step == len(STEPS) - 1
-            if mu:
-                o_sb = osp.tile([P, B * 2 * L], F32, name="o_sb")
-                o5 = o_sb[:].rearrange("p (b c jj r) -> p b c jj r", b=B, c=2, r=R)
-                o4 = o_sb[:].rearrange("p (b c l) -> p b c l", b=B, c=2)
-            for slot in range(6):
-                for h in range(2):
-                    for piece in range(6):
-                        if XPLACE[h][piece] == (step, slot):
-                            x_piece(h, piece)
-                if slot % 2 == 0 and slot < 5 and tu:
-                    w_quant(tu[0], tu[1], slot // 2, groups[slot // 2])
-                if slot % 2 == 1 and slot < 5 and mu:
-                    cc = slot // 2
-                    c = 2 * mu[1] + cc
-                    nc.vector.tensor_tensor(
-                        out=o5[:, :, cc],
-                        in0=accs[cc][:].rearrange("p (r b jj) -> p b jj r", r=R, b=B),
-                        in1=tt4[:, :, c],
-                        op=MULT,
-                    )
-                    if last:
-                        nc.sync.dma_start(out=out_v[mu[0]][:, :, c * L:(c + 1) * L], in_=o4[:, :, cc, :])
-            if mu and not last:
-                nc.sync.dma_start(
-                    out=out_v[mu[0]][:, :, mu[1] * 2 * L:(mu[1] + 1) * 2 * L],
-                    in_=o_sb[:].rearrange("p (b n) -> p b n", b=B),
-                )
+        def way_out(ot, h, cc):
+            o_sb = osp.tile([P, B * L], F32, name="o_sb")
+            c = 2 * h + cc
+            nc.vector.tensor_tensor(
+                out=o_sb[:].rearrange("p (b jj r) -> p b jj r", b=B, r=R),
+                in0=accs[(ot, h, cc)][:].rearrange("p (r b jj) -> p b jj r", r=R, b=B),
+                in1=tt4[:, :, c],
+                op=MULT,
+            )
+            nc.sync.dma_start(out=out_v[ot][:, :, c * L:(c + 1) * L], in_=o_sb[:].rearrange("p (b l) -> p b l", b=B))
+
+        on_vector = [s for s in VSEQ if s[0:2] == "CO"]
+        sseq = ["CO%s%d" % (s[1:3], mi) for s in PESEQ if s[0] == "T" for mi in range(3)]
+        sseq = [s for s in sseq if s not in on_vector]
+
+        def ready(s):
+            kind = s[0:2]
+            if s[0] == "T" or kind == "XR":
+                return True
+            if s[0] == "M":
+                h = int(s[2])
+                need = ["QW%s%d" % (s[1:3], mi) for mi in range(3)] + ["QX%d" % (2 * h), "QX%d" % (2 * h + 1)]
+            elif kind == "CO":
+                need = ["T" + s[2:4]]
+            elif kind == "QW":
+                need = ["CO" + s[2:5]]
+            elif kind == "XE":
+                need = ["XR0" + s[3], "XR1" + s[3]]
+            elif kind == "QX":
+                need = ["XE0%d" % (int(s[2]) // 2), "XE1%d" % (int(s[2]) // 2)]
+            else:
+                need = ["M" + s[2:4]]
+            return all(n in done for n in need)
+
+        def emit(s):
+            kind = s[0:2]
+            if s[0] == "T":
+                transposes(int(s[1]), int(s[2]))
+            elif s[0] == "M":
+                passes(int(s[1]), int(s[2]))
+            elif kind == "CO":
+                copy_out(s in on_vector, int(s[2]), int(s[3]), int(s[4]))
+            elif kind == "QW":
+                w_quant(int(s[2]), int(s[3]), int(s[4]))
+            elif kind == "XR":
+                x_regroup(int(s[2]), int(s[3]))
+            elif kind == "XE":
+                x_edge(int(s[2]), int(s[3]))
+            elif kind == "QX":
+                x_quant(int(s[2]))
+            else:
+                way_out(int(s[2]), int(s[3]), int(s[4]))
+            done.add(s)
+
+        queues = [list(PESEQ), sseq, list(VSEQ)]
+        while any(queues):
+            moved = False
+            for q in queues:
+                while q and ready(q[0]):
+                    emit(q[0])
+                    q[:] = q[1:]
+                    moved = True
+            assert moved

@@ -26,15 +26,13 @@ BANK = 512
 FLOPS = 2 * B * O * C * L * I * KW
 
 LOADS = (("w", 0), ("x", 0), ("w", 1), ("x", 1), ("w", 2), ("w", 3))
-PESEQ = (
-    "T00", "T01", "T10", "M00", "T11", "T20", "M10", "T21", "T30", "M01", "M11", "T31", "M20", "M21", "M30", "M31",
+STEPS = (
+    ((0, 0), None), ((0, 1), None), ((1, 0), (0, 0)), ((1, 1), (1, 0)), ((2, 0), (0, 1)),
+    ((2, 1), (1, 1)), ((3, 0), (2, 0)), ((3, 1), (2, 1)), (None, (3, 0)), (None, (3, 1)),
 )
-VSEQ = (
-    "XR00", "XR10", "QW000", "QW001", "XE00", "XE10", "QW002", "QX0", "QX1", "XR01", "XR11", "EV000", "EV001",
-    "QW100", "QW101", "XE01", "XE11", "QW102", "CO201", "QW010", "QW011", "EV100", "EV101", "QW012", "QX2", "QX3",
-    "QW110", "QW111", "CO301", "QW112", "EV010", "QW200", "EV011", "QW201", "EV110", "QW202", "EV111", "QW210",
-    "QW211", "QW212", "QW300", "QW301", "QW302", "QW310", "EV200", "EV201", "QW311", "EV210", "QW312", "EV211",
-    "EV300", "EV301", "EV310", "EV311",
+XPLACE = (
+    ((0, 0), (0, 0), (0, 2), (0, 2), (0, 4), (0, 5)),
+    ((1, 4), (2, 5), (3, 1), (3, 1), (3, 1), (3, 1)),
 )
 
 
@@ -43,7 +41,7 @@ def tile_timeawareconv1d_kernel(tc, x, time_tensor, weights, out):
     with ExitStack() as ctx:
         ctx.enter_context(tc.manual_schedule())
         keep = ctx.enter_context(tc.tile_pool(name="keep", bufs=1))
-        wgp = ctx.enter_context(tc.tile_pool(name="wgp", bufs=24))
+        wgp = ctx.enter_context(tc.tile_pool(name="wgp", bufs=9))
         osp = ctx.enter_context(tc.tile_pool(name="osp", bufs=8))
         psum = ctx.enter_context(tc.psum_pool(name="psum", bufs=8))
 
@@ -93,63 +91,55 @@ def tile_timeawareconv1d_kernel(tc, x, time_tensor, weights, out):
             else:
                 nc.vector.tensor_copy(out=tt_sb[:, q * BANK:(q + 1) * BANK], in_=tb[:])
 
-        banks = {}
-        groups = {}
-        accs = {}
-        done = set()
-
-        def x_regroup(b, h):
+        def x_piece(h, piece):
             cs = slice(2 * h, 2 * h + 2)
-            for rp in range(0, R, 2):
-                nc.vector.tensor_copy(
-                    out=xg6[:, cs, 1 + rp:3 + rp, b, :, :].rearrange("p c q jj t -> p c jj t q"),
-                    in_=x_raw[b][h][:].rearrange("p (j c jj r) -> p c jj j r", j=PACK, c=2, r=R)[:, :, :, :, rp:rp + 2],
-                )
-
-        def x_edge(side, h):
-            cs = slice(2 * h, 2 * h + 2)
-            if side == 0:
+            if piece < 2:
+                src = x_raw[piece][h][:].rearrange("p (j c jj r) -> p c jj j r", j=PACK, c=2, r=R)
+                for rp in range(0, R, 2):
+                    nc.vector.tensor_copy(
+                        out=xg6[:, cs, 1 + rp:3 + rp, piece, :, :].rearrange("p c q jj t -> p c jj t q"),
+                        in_=src[:, :, :, :, rp:rp + 2],
+                    )
+            elif piece == 2:
                 nc.vector.tensor_copy(out=xg6[:, cs, 0, :, 1:JJ, :], in_=xg6[:, cs, R, :, 0:JJ - 1, :])
-            else:
+            elif piece == 3:
                 nc.vector.tensor_copy(out=xg6[:, cs, PLANES - 1, :, 0:JJ - 1, :], in_=xg6[:, cs, 1, :, 1:JJ, :])
-
-        def x_quant(c):
-            for lo, n in ((0, 512), (512, 256)):
-                a = c * XC + lo
-                nc.vector.quantize_mx(
-                    out=x_codes[:, a:a + n].bitcast(FP8X4),
-                    scales=x_scales[:, a:a + n],
-                    in_=xg[:, a * PACK:(a + n) * PACK],
-                )
+            else:
+                for lo, n in ((0, 512), (512, 256)):
+                    a = (2 * h + piece - 4) * XC + lo
+                    nc.vector.quantize_mx(
+                        out=x_codes[:, a:a + n].bitcast(FP8X4),
+                        scales=x_scales[:, a:a + n],
+                        in_=xg[:, a * PACK:(a + n) * PACK],
+                    )
 
         def transposes(ot, h):
+            banks = []
             for mi in range(3):
                 tp = psum.tile([P, BANK], F32, name="bank")
                 for j in range(PACK):
                     nc.tensor.transpose(
                         out=tp[:, j * P:(j + 1) * P], in_=wv[ot][:, :, j, 3 * h + mi], identity=ident[:]
                     )
-                banks[(ot, h, mi)] = tp
+                banks.append(tp)
+            groups = []
+            for mi in range(3):
+                wg = wgp.tile([P, 2 * P * PACK], BF16, name="wg", align_bytes=64)
+                nc.scalar.copy(
+                    out=wg[:].rearrange("p (e o t) -> p e o t", e=2, t=PACK),
+                    in_=banks[mi][:].bitcast(BF16).rearrange("p (t o e) -> p e o t", t=PACK, e=2),
+                )
+                groups.append(wg)
+            return groups
 
-        def copy_out(on_vector, ot, h, mi):
-            wg = wgp.tile([P, 2 * P * PACK], BF16, name="wg", align_bytes=64)
-            dst = wg[:].rearrange("p (e o t) -> p e o t", e=2, t=PACK)
-            src = banks[(ot, h, mi)][:].bitcast(BF16).rearrange("p (t o e) -> p e o t", t=PACK, e=2)
-            if on_vector:
-                nc.vector.tensor_copy(out=dst, in_=src)
-            else:
-                nc.scalar.copy(out=dst, in_=src)
-            groups[(ot, h, mi)] = wg
-
-        def w_quant(ot, h, mi):
+        def w_quant(ot, h, mi, wg):
             a = (ot * CK + 2 * (3 * h + mi)) * P
             nc.vector.quantize_mx(
-                out=w_codes[:, a:a + 2 * P].bitcast(FP8X4),
-                scales=w_scales[:, a:a + 2 * P],
-                in_=groups[(ot, h, mi)][:],
+                out=w_codes[:, a:a + 2 * P].bitcast(FP8X4), scales=w_scales[:, a:a + 2 * P], in_=wg[:]
             )
 
         def passes(ot, h):
+            accs = []
             for cc in range(2):
                 c = 2 * h + cc
                 acc = psum.tile([P, BANK], F32, name="bank")
@@ -165,68 +155,28 @@ def tile_timeawareconv1d_kernel(tc, x, time_tensor, weights, out):
                         start=(k == 0),
                         stop=(k == KW - 1),
                     )
-                accs[(ot, h, cc)] = acc
+                accs.append(acc)
+            return accs
 
-        def way_out(ot, h, cc):
+        def way_out(ot, c, acc):
             o_sb = osp.tile([P, B * L], F32, name="o_sb")
-            c = 2 * h + cc
             nc.vector.tensor_tensor(
                 out=o_sb[:].rearrange("p (b jj r) -> p b jj r", b=B, r=R),
-                in0=accs[(ot, h, cc)][:].rearrange("p (r b jj) -> p b jj r", r=R, b=B),
+                in0=acc[:].rearrange("p (r b jj) -> p b jj r", r=R, b=B),
                 in1=tt4[:, :, c],
                 op=MULT,
             )
             nc.sync.dma_start(out=out_v[ot][:, :, c * L:(c + 1) * L], in_=o_sb[:].rearrange("p (b l) -> p b l", b=B))
 
-        on_vector = [s for s in VSEQ if s[0:2] == "CO"]
-        sseq = ["CO%s%d" % (s[1:3], mi) for s in PESEQ if s[0] == "T" for mi in range(3)]
-        sseq = [s for s in sseq if s not in on_vector]
-
-        def ready(s):
-            kind = s[0:2]
-            if s[0] == "T" or kind == "XR":
-                return True
-            if s[0] == "M":
-                h = int(s[2])
-                need = ["QW%s%d" % (s[1:3], mi) for mi in range(3)] + ["QX%d" % (2 * h), "QX%d" % (2 * h + 1)]
-            elif kind == "CO":
-                need = ["T" + s[2:4]]
-            elif kind == "QW":
-                need = ["CO" + s[2:5]]
-            elif kind == "XE":
-                need = ["XR0" + s[3], "XR1" + s[3]]
-            elif kind == "QX":
-                need = ["XE0%d" % (int(s[2]) // 2), "XE1%d" % (int(s[2]) // 2)]
-            else:
-                need = ["M" + s[2:4]]
-            return all(n in done for n in need)
-
-        def emit(s):
-            kind = s[0:2]
-            if s[0] == "T":
-                transposes(int(s[1]), int(s[2]))
-            elif s[0] == "M":
-                passes(int(s[1]), int(s[2]))
-            elif kind == "CO":
-                copy_out(s in on_vector, int(s[2]), int(s[3]), int(s[4]))
-            elif kind == "QW":
-                w_quant(int(s[2]), int(s[3]), int(s[4]))
-            elif kind == "XR":
-                x_regroup(int(s[2]), int(s[3]))
-            elif kind == "XE":
-                x_edge(int(s[2]), int(s[3]))
-            elif kind == "QX":
-                x_quant(int(s[2]))
-            else:
-                way_out(int(s[2]), int(s[3]), int(s[4]))
-            done.add(s)
-
-        queues = [list(PESEQ), sseq, list(VSEQ)]
-        while any(queues):
-            moved = False
-            for q in queues:
-                while q and ready(q[0]):
-                    emit(q[0])
-                    q[:] = q[1:]
-                    moved = True
-            assert moved
+        for step, (tu, mu) in enumerate(STEPS):
+            groups = transposes(tu[0], tu[1]) if tu else None
+            accs = passes(mu[0], mu[1]) if mu else None
+            for slot in range(6):
+                for h in range(2):
+                    for piece in range(6):
+                        if XPLACE[h][piece] == (step, slot):
+                            x_piece(h, piece)
+                if slot % 2 == 0 and slot < 5 and tu:
+                    w_quant(tu[0], tu[1], slot // 2, groups[slot // 2])
+                if slot % 2 == 1 and slot < 5 and mu:
+                    way_out(mu[0], 2 * mu[1] + slot // 2, accs[slot // 2])

from contextlib import ExitStack

import concourse.mybir as mybir
from concourse.masks import make_identity

F32 = mybir.dt.float32
BF16 = mybir.dt.bfloat16
I32 = mybir.dt.int32
U32 = mybir.dt.uint32
U8 = mybir.dt.uint8
FP8X4 = mybir.dt.float8_e4m3fn_x4
MULT = mybir.AluOpType.mult

B, I, C, L, O, KW = 2, 512, 4, 256, 512, 3
P = 128
PACK = 4
NOT = O // P
CK = C * KW
PAIRS = CK // 2
R = 4
JJ = L // R
PLANES = R + 2
PLANE_COLS = B * JJ
XC = PLANES * PLANE_COLS
BANK = 512
FLOPS = 2 * B * O * C * L * I * KW

LOADS = (("w", 0), ("x", 0), ("w", 1), ("x", 1), ("w", 2), ("w", 3))
STEPS = (
    ((0, 0), None), ((0, 1), None), ((1, 0), (0, 0)), ((1, 1), (1, 0)), ((2, 0), (0, 1)),
    ((2, 1), (1, 1)), ((3, 0), (2, 0)), ((3, 1), (2, 1)), (None, (3, 0)), (None, (3, 1)),
)
XPLACE = (
    ((0, 0), (0, 0), (0, 2), (0, 2), (0, 4), (0, 5)),
    ((1, 4), (2, 5), (3, 1), (3, 1), (3, 1), (3, 1)),
)


def tile_timeawareconv1d_kernel(tc, x, time_tensor, weights, out):
    nc = tc.nc
    with ExitStack() as ctx:
        ctx.enter_context(tc.manual_schedule())
        keep = ctx.enter_context(tc.tile_pool(name="keep", bufs=1))
        wgp = ctx.enter_context(tc.tile_pool(name="wgp", bufs=9))
        osp = ctx.enter_context(tc.tile_pool(name="osp", bufs=8))
        psum = ctx.enter_context(tc.psum_pool(name="psum", bufs=8))

        w_raw = [keep.tile([P, I * CK], BF16, name="w_raw%d" % ot) for ot in range(NOT)]
        x_raw = [[keep.tile([P, PACK * 2 * L], BF16, name="x_raw%d%d" % (b, h)) for h in range(2)] for b in range(B)]
        xg = keep.tile([P, C * XC * PACK], BF16, align_bytes=64)
        x_codes = keep.tile([P, C * XC], U32, align_bytes=64)
        x_scales = keep.tile([P, C * XC], U8, align_bytes=64)
        w_codes = keep.tile([P, NOT * CK * P], U32, align_bytes=64)
        w_scales = keep.tile([P, NOT * CK * P], U8, align_bytes=64)
        tt_row = keep.tile([P, B * C * L], BF16)
        tt_sb = keep.tile([P, B * C * L], BF16)
        sel = keep.tile([P, P], BF16)
        ident = keep.tile([P, P], F32)

        xg6 = xg[:].rearrange("p (c q b jj t) -> p c q b jj t", c=C, q=PLANES, b=B, t=PACK)
        wv = [w_raw[ot][:].bitcast(F32).rearrange("o (p j m) -> o p j m", j=PACK, m=PAIRS) for ot in range(NOT)]
        tt4 = tt_sb[:].rearrange("p (b c jj r) -> p b c jj r", b=B, c=C, r=R)
        out_v = out.rearrange("b (t p) c l -> t p b (c l)", p=P)

        nc.sync.dma_start(out=tt_row[0:32, :], in_=time_tensor.rearrange("b c l -> (b c l)").partition_broadcast(32))
        for kind, n in LOADS:
            if kind == "w":
                nc.sync.dma_start(
                    out=w_raw[n][:], in_=weights[n * P:(n + 1) * P].rearrange("o i c k -> o (i c k)")
                )
            else:
                for b in range(B):
                    nc.sync.dma_start(
                        out=x_raw[b][n][:].rearrange("p (j n) -> p j n", j=PACK),
                        in_=x[b].rearrange("(p j) c l -> p j c l", j=PACK)[:, :, 2 * n:2 * n + 2, :].rearrange(
                            "p j c l -> p j (c l)"
                        ),
                    )
        nc.vector.memset(tt_row[32:64, :].bitcast(I32), 0)
        nc.vector.memset(tt_row[64:128, :].bitcast(I32), 0)
        nc.vector.memset(sel[:], 0.0)
        nc.vector.memset(sel[0:1, :], 1.0)
        make_identity(nc, ident[:])
        nc.vector.memset(xg6[:, :, 0, :, 0, :], 0.0)
        nc.vector.memset(xg6[:, :, PLANES - 1, :, JJ - 1, :], 0.0)
        for q in range(B * C * L // BANK):
            tb = psum.tile([P, BANK], F32, name="bank")
            nc.tensor.matmul(out=tb[:], lhsT=sel[:], rhs=tt_row[:, q * BANK:(q + 1) * BANK], start=True, stop=True)
            if q % 2 == 0:
                nc.scalar.copy(out=tt_sb[:, q * BANK:(q + 1) * BANK], in_=tb[:])
            else:
                nc.vector.tensor_copy(out=tt_sb[:, q * BANK:(q + 1) * BANK], in_=tb[:])

        def x_piece(h, piece):
            cs = slice(2 * h, 2 * h + 2)
            if piece < 2:
                src = x_raw[piece][h][:].rearrange("p (j c jj r) -> p c jj j r", j=PACK, c=2, r=R)
                for rp in range(0, R, 2):
                    nc.vector.tensor_copy(
                        out=xg6[:, cs, 1 + rp:3 + rp, piece, :, :].rearrange("p c q jj t -> p c jj t q"),
                        in_=src[:, :, :, :, rp:rp + 2],
                    )
            elif piece == 2:
                nc.vector.tensor_copy(out=xg6[:, cs, 0, :, 1:JJ, :], in_=xg6[:, cs, R, :, 0:JJ - 1, :])
            elif piece == 3:
                nc.vector.tensor_copy(out=xg6[:, cs, PLANES - 1, :, 0:JJ - 1, :], in_=xg6[:, cs, 1, :, 1:JJ, :])
            else:
                for lo, n in ((0, 512), (512, 256)):
                    a = (2 * h + piece - 4) * XC + lo
                    nc.vector.quantize_mx(
                        out=x_codes[:, a:a + n].bitcast(FP8X4),
                        scales=x_scales[:, a:a + n],
                        in_=xg[:, a * PACK:(a + n) * PACK],
                    )

        def transposes(ot, h):
            banks = []
            for mi in range(3):
                tp = psum.tile([P, BANK], F32, name="bank")
                for j in range(PACK):
                    nc.tensor.transpose(
                        out=tp[:, j * P:(j + 1) * P], in_=wv[ot][:, :, j, 3 * h + mi], identity=ident[:]
                    )
                banks.append(tp)
            groups = []
            for mi in range(3):
                wg = wgp.tile([P, 2 * P * PACK], BF16, name="wg", align_bytes=64)
                nc.scalar.copy(
                    out=wg[:].rearrange("p (e o t) -> p e o t", e=2, t=PACK),
                    in_=banks[mi][:].bitcast(BF16).rearrange("p (t o e) -> p e o t", t=PACK, e=2),
                )
                groups.append(wg)
            return groups

        def w_quant(ot, h, mi, wg):
            a = (ot * CK + 2 * (3 * h + mi)) * P
            nc.vector.quantize_mx(
                out=w_codes[:, a:a + 2 * P].bitcast(FP8X4), scales=w_scales[:, a:a + 2 * P], in_=wg[:]
            )

        def passes(ot, h):
            accs = []
            for cc in range(2):
                c = 2 * h + cc
                acc = psum.tile([P, BANK], F32, name="bank")
                for k in range(KW):
                    a = (ot * CK + c * KW + k) * P
                    xa = c * XC + k * PLANE_COLS
                    nc.tensor.matmul_mx(
                        out=acc[:],
                        lhsT=w_codes[:, a:a + P].bitcast(FP8X4),
                        lhsT_scale=w_scales[:, a:a + P],
                        rhs=x_codes[:, xa:xa + BANK].bitcast(FP8X4),
                        rhs_scale=x_scales[:, xa:xa + BANK],
                        start=(k == 0),
                        stop=(k == KW - 1),
                    )
                accs.append(acc)
            return accs

        def way_out(ot, c, acc):
            o_sb = osp.tile([P, B * L], F32, name="o_sb")
            nc.vector.tensor_tensor(
                out=o_sb[:].rearrange("p (b jj r) -> p b jj r", b=B, r=R),
                in0=acc[:].rearrange("p (r b jj) -> p b jj r", r=R, b=B),
                in1=tt4[:, :, c],
                op=MULT,
            )
            nc.sync.dma_start(out=out_v[ot][:, :, c * L:(c + 1) * L], in_=o_sb[:].rearrange("p (b l) -> p b l", b=B))

        for step, (tu, mu) in enumerate(STEPS):
            groups = transposes(tu[0], tu[1]) if tu else None
            accs = passes(mu[0], mu[1]) if mu else None
            for slot in range(6):
                for h in range(2):
                    for piece in range(6):
                        if XPLACE[h][piece] == (step, slot):
                            x_piece(h, piece)
                if slot % 2 == 0 and slot < 5 and tu:
                    w_quant(tu[0], tu[1], slot // 2, groups[slot // 2])
                if slot % 2 == 1 and slot < 5 and mu:
                    way_out(mu[0], 2 * mu[1] + slot // 2, accs[slot // 2])
